import numpy as np
import ml_dtypes


def mxq(x, axis, fmt="e4m3"):
    dtype, down = {"e4m3": (ml_dtypes.float8_e4m3fn, 7), "e5m2": (ml_dtypes.float8_e5m2, 14)}[fmt]
    v = np.moveaxis(np.asarray(x, np.float32).astype(ml_dtypes.bfloat16).astype(np.float64), axis, -1)
    blocks = v.reshape(v.shape[:-1] + (-1, 32))
    amax = np.abs(blocks).max(-1, keepdims=True)
    byte = np.maximum(np.where(amax > 0, np.frexp(amax)[1] - 1 + 127, 0) - down, 1)
    scale = np.exp2(byte - 127.0)
    codes = (blocks / scale).astype(np.float32).astype(dtype).astype(np.float64)
    return np.moveaxis((codes * scale).reshape(v.shape), -1, axis)


WIDE = False


def mx_kscale(k):
    if not WIDE:
        return np.ones(k)
    levels = np.array([10, -10, 5, -5, 0])
    a = np.random.permutation(np.resize(levels, k // 512 * 4)).reshape(k // 512, 4)
    idx = np.arange(k)
    return np.exp2(a[idx // 512, idx % 128 // 32])


BF16 = ml_dtypes.bfloat16


def bf(x):
    return np.asarray(x, np.float32).astype(BF16)


def f64(x):
    return np.asarray(x).astype(np.float64)


B, T, C, H, QB = 32, 512, 512, 128, 512
GAMMA = 0.96875


def decay(n0, n1, m1):
    dist = np.arange(n0, n1)[:, None] - np.arange(m1)[None, :]
    return np.where(dist >= 0, GAMMA ** f64(np.maximum(dist, 0)), 0.0)


def setup_inputs():
    s, f = mx_kscale(C), mx_kscale(T)
    return {"q": bf(np.random.standard_normal((B, T, H))),
            "k": bf(np.random.standard_normal((B, T, H)) * f[:, None]),
            "x": bf(np.random.standard_normal((B, T, C)) * s / f[:, None]),
            "Wv": bf(np.random.standard_normal((C, H)) / np.sqrt(C) / s[:, None])}


def reference(q, k, x, Wv):
    q, k = f64(q), f64(k)
    v = mxq(f64(x), 2, "e4m3") @ mxq(f64(Wv), 0, "e4m3")
    vq = mxq(v, 1, "e4m3")
    scale = C ** -0.5
    rows = []
    for n0 in range(0, T, QB):
        n1 = n0 + QB
        wei = q[:, n0:n1] @ k[:, :n1].transpose(0, 2, 1) * scale * decay(n0, n1, n1)
        rows.append(mxq(wei, 2, "e4m3") @ vq[:, :n1])
    return np.concatenate(rows, axis=1)

@@ -1,0 +1,239 @@
+from contextlib import ExitStack
+import math
+
+import concourse.mybir as mybir
+from concourse.masks import make_identity
+
+F32 = mybir.dt.float32
+BF16 = mybir.dt.bfloat16
+U8 = mybir.dt.uint8
+U32 = mybir.dt.uint32
+I32 = mybir.dt.int32
+FP8X4 = mybir.dt.float8_e4m3fn_x4
+ALU = mybir.AluOpType
+ACT = mybir.ActivationFunctionType
+
+B, T, C, H = 32, 512, 512, 128
+P = 128
+GAMMA = 0.96875
+FLOPS = 3 * 2 * B * T * T * H
+PIN = True
+AHEAD = 2
+TAB_OFF = (0, 128, 384, 768)
+
+
+def tile_retentionhead_pa_t_kernel(tc, q, k, x, Wv, out):
+    nc = tc.nc
+    with ExitStack() as ctx:
+        const = ctx.enter_context(tc.tile_pool(name="const", bufs=1))
+        loads = ctx.enter_context(tc.tile_pool(name="loads", bufs=AHEAD + 2))
+        work = ctx.enter_context(tc.tile_pool(name="work", bufs=2))
+        outs = ctx.enter_context(tc.tile_pool(name="outs", bufs=3))
+        psum = ctx.enter_context(tc.psum_pool(name="psum", bufs=1))
+        if PIN:
+            ctx.enter_context(tc.manual_schedule())
+
+        x_in, q_in, k_in = {}, {}, {}
+
+        def load_pair(g):
+            kt = loads.tile([P, 2 * 512], BF16, name="kt", tag="kt")
+            qt = loads.tile([P, 2 * 512], BF16, name="qt", tag="qt")
+            xt = loads.tile([P, 2 * 2048], BF16, name="xt", tag="xt")
+            bs = slice(2 * g, 2 * g + 2)
+            nc.sync.dma_start(
+                out=kt[:].rearrange("p (b t h) -> p b t h", b=2, t=4),
+                in_=k[bs].rearrange("b (t p) h -> p b t h", p=P),
+            )
+            nc.sync.dma_start(
+                out=qt[:].rearrange("p (b w) -> p b w", b=2),
+                in_=q[bs].rearrange("b (p j) h -> p b (j h)", j=4),
+            )
+            nc.sync.dma_start(
+                out=xt[:].rearrange("p (b w) -> p b w", b=2),
+                in_=x[bs].rearrange("b (p j) c -> p b (j c)", j=4),
+            )
+            k_in[g], q_in[g], x_in[g] = kt, qt, xt
+
+        load_pair(0)
+        wv_sb = const.tile([P, 4, H], BF16, name="wv_sb")
+        nc.sync.dma_start(
+            out=wv_sb[:].rearrange("q (u e) h -> q u e h", u=2),
+            in_=Wv.rearrange("(u q e) h -> q u e h", u=2, e=2),
+        )
+        for g in range(1, AHEAD + 1):
+            load_pair(g)
+
+        d_int = const.tile([P, P], I32, name="d_int")
+        nc.gpsimd.iota(out=d_int[:], pattern=[[1, 4], [4, 32]], base=0, channel_multiplier=-1)
+        ident_b = const.tile([P, P], BF16, name="ident_b")
+        make_identity(nc, ident_b[:])
+        ident_f = const.tile([P, P], F32, name="ident_f")
+        make_identity(nc, ident_f[:])
+
+        gw = []
+        for s in range(2):
+            g_t = const.tile([P, 2048], BF16, name="gw%d" % s, align_bytes=64)
+            nc.vector.memset(g_t[:].bitcast(I32), 0)
+            gw.append(g_t)
+        off4 = const.tile([P, 4], F32, name="off4")
+        for s in range(4):
+            nc.vector.memset(off4[:, s : s + 1], 128.0 * (3 - s))
+        d_f = const.tile([P, P], F32, name="d_f")
+        nc.vector.tensor_copy(out=d_f[:], in_=d_int[:])
+        dist = const.tile([P, 1280], F32, name="dist")
+        for jn in range(4):
+            n = jn + 1
+            nc.vector.tensor_tensor(
+                out=dist[:, TAB_OFF[jn] : TAB_OFF[jn] + P * n].rearrange("p (w t) -> p w t", t=n),
+                in0=d_f[:].unsqueeze(2).to_broadcast([P, P, n]),
+                in1=off4[:, 3 - jn : 4].unsqueeze(1).to_broadcast([P, P, n]),
+                op=ALU.add,
+            )
+        powers = const.tile([P, 1280], F32, name="powers")
+        nc.scalar.activation(out=powers[:], in_=dist[:], func=ACT.Exp, scale=math.log(GAMMA))
+        mask = const.tile([P, 1280], F32, name="mask")
+        nc.vector.tensor_scalar(
+            out=mask[:], in0=dist[:], scalar1=0.0, scalar2=C**-0.5, op0=ALU.is_ge, op1=ALU.mult
+        )
+        tab = const.tile([P, 1280], F32, name="tab")
+        nc.vector.tensor_tensor(out=tab[:], in0=powers[:], in1=mask[:], op=ALU.mult)
+
+        g_wv = const.tile([P, H, 4], BF16, name="g_wv", align_bytes=64)
+        nc.vector.tensor_copy(out=g_wv[:], in_=wv_sb[:].rearrange("q t h -> q h t"))
+        wv_q = const.tile([P, H], U32, name="wv_q", align_bytes=64)
+        wv_s = const.tile([P, H], U8, name="wv_s", align_bytes=64)
+        nc.vector.quantize_mx(
+            out=wv_q[:].bitcast(FP8X4), scales=wv_s[:], in_=g_wv[:].rearrange("q h t -> q (h t)")
+        )
+
+        qkT, gx, xq, xs, gv, vq, vs, wq, ws, s_ps = {}, {}, {}, {}, {}, {}, {}, {}, {}, {}
+
+        def transposes(b):
+            g, r = divmod(b, 2)
+            qk_ps = psum.tile([P, 8, P], BF16, name="qk_ps", tag="qk")
+            for t in range(4):
+                nc.tensor.transpose(
+                    out=qk_ps[:, t, :], in_=k_in[g][:, r * 512 + t * P : r * 512 + (t + 1) * P], identity=ident_b[:]
+                )
+            for j in range(4):
+                nc.tensor.transpose(
+                    out=qk_ps[:, 4 + j, :], in_=q_in[g][:, r * 512 + j * P : r * 512 + (j + 1) * P], identity=ident_b[:]
+                )
+            qkT[b] = work.tile([P, 8, P], BF16, name="qkT", tag="qkT")
+            nc.scalar.copy(out=qkT[b][:], in_=qk_ps[:])
+            xw = x_in[g][:].bitcast(F32)
+            gx[b] = work.tile([P, 2048], BF16, name="gx", tag="gx", align_bytes=64)
+            gxw = gx[b][:].bitcast(F32).rearrange("c (p hf s) -> c hf p s", hf=2, s=4)
+            for hf in range(2):
+                x_ps = psum.tile([P, 4, P], F32, name="x_ps%d" % hf, tag="x%d" % hf)
+                for s in range(4):
+                    j, u = 2 * hf + s // 2, s % 2
+                    o = r * 1024 + j * 256 + u * P
+                    nc.tensor.transpose(out=x_ps[:, s, :], in_=xw[:, o : o + P], identity=ident_f[:])
+                nc.scalar.copy(out=gxw[:, hf], in_=x_ps[:].rearrange("c s p -> c p s"))
+
+        def quant_x(b):
+            xq[b] = work.tile([P, 512], U32, name="xq", tag="xq", align_bytes=64)
+            xs[b] = work.tile([P, 512], U8, name="xs", tag="xs", align_bytes=64)
+            nc.vector.quantize_mx(out=xq[b][:].bitcast(FP8X4), scales=xs[b][:], in_=gx[b][:])
+
+        S_SLOT = {3: ("sa", 0), 2: ("sb", 0), 0: ("sb", 3), 1: ("sc", 0)}
+
+        def scores(b, jns):
+            for jn in jns:
+                tag, first = S_SLOT[jn]
+                if (b, tag) not in s_ps:
+                    s_ps[(b, tag)] = psum.tile([P, 4, P], F32, name="s_" + tag, tag=tag)
+                bank = s_ps[(b, tag)]
+                for t in range(jn + 1):
+                    nc.tensor.matmul(
+                        out=bank[:, first + t, :].rearrange("p (j i) -> p j i", j=4),
+                        lhsT=qkT[b][:, t, :],
+                        rhs=qkT[b][:, 4:8, 32 * jn : 32 * jn + 32],
+                        start=True,
+                        stop=True,
+                    )
+
+        def weigh(b, jn):
+            tag, first = S_SLOT[jn]
+            n = jn + 1
+            nc.vector.tensor_tensor(
+                out=gw[b % 2][:].rearrange("p (j i t) -> p j i t", j=4, t=4)[:, :, 32 * jn : 32 * jn + 32, 0:n],
+                in0=s_ps[(b, tag)][:, first : first + n, :].rearrange("p t (j i) -> p j i t", j=4),
+                in1=tab[:, TAB_OFF[jn] : TAB_OFF[jn] + P * n].rearrange("p (j i t) -> p j i t", j=4, t=n),
+                op=ALU.mult,
+            )
+
+        def quant_w(b):
+            wq[b] = work.tile([P, 512], U32, name="wq", tag="wq", align_bytes=64)
+            ws[b] = work.tile([P, 512], U8, name="ws", tag="ws", align_bytes=64)
+            nc.vector.quantize_mx(out=wq[b][:].bitcast(FP8X4), scales=ws[b][:], in_=gw[b % 2][:])
+
+        def values(b):
+            v_ps = psum.tile([P, 4, H], F32, name="v_ps", tag="v")
+            for t in range(4):
+                cols = slice(t * P, (t + 1) * P)
+                nc.tensor.matmul_mx(
+                    out=v_ps[:, t, :],
+                    lhsT=xq[b][:, cols].bitcast(FP8X4),
+                    lhsT_scale=xs[b][:, cols],
+                    rhs=wv_q[:].bitcast(FP8X4),
+                    rhs_scale=wv_s[:],
+                    start=True,
+                    stop=True,
+                )
+            gv[b] = work.tile([P, H, 4], BF16, name="gv", tag="gv", align_bytes=64)
+            nc.scalar.copy(out=gv[b][:], in_=v_ps[:].rearrange("p t h -> p h t"))
+
+        def quant_v(b):
+            vq[b] = work.tile([P, H], U32, name="vq", tag="vq", align_bytes=64)
+            vs[b] = work.tile([P, H], U8, name="vs", tag="vs", align_bytes=64)
+            nc.vector.quantize_mx(
+                out=vq[b][:].bitcast(FP8X4), scales=vs[b][:], in_=gv[b][:].rearrange("p h t -> p (h t)")
+            )
+
+        def outputs(b):
+            o_ps = psum.tile([P, 4, H], F32, name="o_ps", tag="o")
+            for j in range(4):
+                cols = slice(j * P, (j + 1) * P)
+                nc.tensor.matmul_mx(
+                    out=o_ps[:, j, :],
+                    lhsT=wq[b][:, cols].bitcast(FP8X4),
+                    lhsT_scale=ws[b][:, cols],
+                    rhs=vq[b][:].bitcast(FP8X4),
+                    rhs_scale=vs[b][:],
+                    start=True,
+                    stop=True,
+                )
+            o_sb = outs.tile([P, 4, H], F32, name="o_sb", tag="o_sb")
+            nc.scalar.copy(out=o_sb[:], in_=o_ps[:])
+            nc.sync.dma_start(out=out[b].rearrange("(i j) h -> i j h", j=4), in_=o_sb[:])
+
+        def on(b):
+            return 0 <= b < B
+
+        for i in range(-2, B + 1):
+            if on(i - 1):
+                outputs(i - 1)
+            if on(i):
+                values(i)
+                weigh(i, 3)
+            if on(i + 1):
+                scores(i + 1, (3,))
+            if on(i + 2):
+                if (i + 2) % 2 == 0 and (i + 2) // 2 + AHEAD < B // 2 and (i + 2) // 2 > 0:
+                    load_pair((i + 2) // 2 + AHEAD)
+                transposes(i + 2)
+            if on(i):
+                weigh(i, 2)
+                weigh(i, 0)
+            if on(i + 1):
+                scores(i + 1, (2, 0))
+            if on(i):
+                weigh(i, 1)
+            if on(i + 1):
+                scores(i + 1, (1,))
+                quant_x(i + 1)
+            if on(i):
+                quant_v(i)
+                quant_w(i)

@@ -48,10 +48,16 @@ def tile_retentionhead_pa_t_kernel(tc, q, k, x, Wv, out):
                 out=qt[:].rearrange("p (b w) -> p b w", b=2),
                 in_=q[bs].rearrange("b (p j) h -> p b (j h)", j=4),
             )
-            nc.sync.dma_start(
-                out=xt[:].rearrange("p (b w) -> p b w", b=2),
-                in_=x[bs].rearrange("b (p j) c -> p b (j c)", j=4),
-            )
+            if g == 0:
+                for r in range(2):
+                    nc.sync.dma_start(
+                        out=xt[:, r * 2048 : (r + 1) * 2048], in_=x[r].rearrange("(p j) c -> p (j c)", j=4)
+                    )
+            else:
+                nc.sync.dma_start(
+                    out=xt[:].rearrange("p (b w) -> p b w", b=2),
+                    in_=x[bs].rearrange("b (p j) c -> p b (j c)", j=4),
+                )
             k_in[g], q_in[g], x_in[g] = kt, qt, xt
 
         load_pair(0)
@@ -63,6 +69,10 @@ def tile_retentionhead_pa_t_kernel(tc, q, k, x, Wv, out):
         for g in range(1, AHEAD + 1):
             load_pair(g)
 
+        warm_in = const.tile([P, 1], F32, name="warm_in")
+        warm_out = const.tile([P, 1], F32, name="warm_out")
+        nc.vector.memset(warm_in[:], 0.0)
+        nc.scalar.activation(out=warm_out[:], in_=warm_in[:], func=ACT.Exp)
         d_int = const.tile([P, P], I32, name="d_int")
         nc.gpsimd.iota(out=d_int[:], pattern=[[1, 4], [4, 32]], base=0, channel_multiplier=-1)
         ident_b = const.tile([P, P], BF16, name="ident_b")
@@ -70,33 +80,32 @@ def tile_retentionhead_pa_t_kernel(tc, q, k, x, Wv, out):
         ident_f = const.tile([P, P], F32, name="ident_f")
         make_identity(nc, ident_f[:])
 
-        gw = []
-        for s in range(2):
-            g_t = const.tile([P, 2048], BF16, name="gw%d" % s, align_bytes=64)
-            nc.vector.memset(g_t[:].bitcast(I32), 0)
-            gw.append(g_t)
         off4 = const.tile([P, 4], F32, name="off4")
         for s in range(4):
             nc.vector.memset(off4[:, s : s + 1], 128.0 * (3 - s))
         d_f = const.tile([P, P], F32, name="d_f")
         nc.vector.tensor_copy(out=d_f[:], in_=d_int[:])
         dist = const.tile([P, 1280], F32, name="dist")
-        for jn in range(4):
+        powers = const.tile([P, 1280], F32, name="powers")
+        mask = const.tile([P, 1280], F32, name="mask")
+        tab = const.tile([P, 1280], F32, name="tab")
+        gw = const.tile([P, 2048], BF16, name="gw", align_bytes=64)
+        for jn in (3, 2, 1, 0):
             n = jn + 1
+            sl = slice(TAB_OFF[jn], TAB_OFF[jn] + P * n)
             nc.vector.tensor_tensor(
-                out=dist[:, TAB_OFF[jn] : TAB_OFF[jn] + P * n].rearrange("p (w t) -> p w t", t=n),
+                out=dist[:, sl].rearrange("p (w t) -> p w t", t=n),
                 in0=d_f[:].unsqueeze(2).to_broadcast([P, P, n]),
                 in1=off4[:, 3 - jn : 4].unsqueeze(1).to_broadcast([P, P, n]),
                 op=ALU.add,
             )
-        powers = const.tile([P, 1280], F32, name="powers")
-        nc.scalar.activation(out=powers[:], in_=dist[:], func=ACT.Exp, scale=math.log(GAMMA))
-        mask = const.tile([P, 1280], F32, name="mask")
-        nc.vector.tensor_scalar(
-            out=mask[:], in0=dist[:], scalar1=0.0, scalar2=C**-0.5, op0=ALU.is_ge, op1=ALU.mult
-        )
-        tab = const.tile([P, 1280], F32, name="tab")
-        nc.vector.tensor_tensor(out=tab[:], in0=powers[:], in1=mask[:], op=ALU.mult)
+            nc.scalar.activation(out=powers[:, sl], in_=dist[:, sl], func=ACT.Exp, scale=math.log(GAMMA))
+            nc.vector.tensor_scalar(
+                out=mask[:, sl], in0=dist[:, sl], scalar1=0.0, scalar2=C**-0.5, op0=ALU.is_ge, op1=ALU.mult
+            )
+            if jn == 3:
+                nc.vector.memset(gw[:].bitcast(I32), 0)
+            nc.vector.tensor_tensor(out=tab[:, sl], in0=powers[:, sl], in1=mask[:, sl], op=ALU.mult)
 
         g_wv = const.tile([P, H, 4], BF16, name="g_wv", align_bytes=64)
         nc.vector.tensor_copy(out=g_wv[:], in_=wv_sb[:].rearrange("q t h -> q h t"))
@@ -108,7 +117,7 @@ def tile_retentionhead_pa_t_kernel(tc, q, k, x, Wv, out):
 
         qkT, gx, xq, xs, gv, vq, vs, wq, ws, s_ps = {}, {}, {}, {}, {}, {}, {}, {}, {}, {}
 
-        def transposes(b):
+        def transposes_qk(b):
             g, r = divmod(b, 2)
             qk_ps = psum.tile([P, 8, P], BF16, name="qk_ps", tag="qk")
             for t in range(4):
@@ -121,6 +130,9 @@ def tile_retentionhead_pa_t_kernel(tc, q, k, x, Wv, out):
                 )
             qkT[b] = work.tile([P, 8, P], BF16, name="qkT", tag="qkT")
             nc.scalar.copy(out=qkT[b][:], in_=qk_ps[:])
+
+        def transposes_x(b):
+            g, r = divmod(b, 2)
             xw = x_in[g][:].bitcast(F32)
             gx[b] = work.tile([P, 2048], BF16, name="gx", tag="gx", align_bytes=64)
             gxw = gx[b][:].bitcast(F32).rearrange("c (p hf s) -> c hf p s", hf=2, s=4)
@@ -137,7 +149,8 @@ def tile_retentionhead_pa_t_kernel(tc, q, k, x, Wv, out):
             xs[b] = work.tile([P, 512], U8, name="xs", tag="xs", align_bytes=64)
             nc.vector.quantize_mx(out=xq[b][:].bitcast(FP8X4), scales=xs[b][:], in_=gx[b][:])
 
-        S_SLOT = {3: ("sa", 0), 2: ("sb", 0), 0: ("sb", 3), 1: ("sc", 0)}
+        S_SLOT = {3: ("sa", 0), 2: ("sb", 0), 1: ("sc", 0)}
+        s0_sb = {}
 
         def scores(b, jns):
             for jn in jns:
@@ -154,11 +167,31 @@ def tile_retentionhead_pa_t_kernel(tc, q, k, x, Wv, out):
                         stop=True,
                     )
 
+        def scores0(b):
+            s0_ps = psum.tile([P, P], F32, name="s0_ps", tag="o")
+            nc.tensor.matmul(
+                out=s0_ps[:].rearrange("p (j i) -> p j i", j=4),
+                lhsT=qkT[b][:, 0, :],
+                rhs=qkT[b][:, 4:8, 0:32],
+                start=True,
+                stop=True,
+            )
+            s0_sb[b] = work.tile([P, P], F32, name="s0_sb", tag="s0_sb")
+            nc.scalar.copy(out=s0_sb[b][:], in_=s0_ps[:])
+
+        def weigh0(b):
+            nc.gpsimd.tensor_tensor(
+                out=gw[:].rearrange("p (j i t) -> p j i t", j=4, t=4)[:, :, 0:32, 0:1],
+                in0=s0_sb[b][:].rearrange("p (j i t) -> p j i t", j=4, t=1),
+                in1=tab[:, 0:P].rearrange("p (j i t) -> p j i t", j=4, t=1),
+                op=ALU.mult,
+            )
+
         def weigh(b, jn):
             tag, first = S_SLOT[jn]
             n = jn + 1
             nc.vector.tensor_tensor(
-                out=gw[b % 2][:].rearrange("p (j i t) -> p j i t", j=4, t=4)[:, :, 32 * jn : 32 * jn + 32, 0:n],
+                out=gw[:].rearrange("p (j i t) -> p j i t", j=4, t=4)[:, :, 32 * jn : 32 * jn + 32, 0:n],
                 in0=s_ps[(b, tag)][:, first : first + n, :].rearrange("p t (j i) -> p j i t", j=4),
                 in1=tab[:, TAB_OFF[jn] : TAB_OFF[jn] + P * n].rearrange("p (j i t) -> p j i t", j=4, t=n),
                 op=ALU.mult,
@@ -167,7 +200,7 @@ def tile_retentionhead_pa_t_kernel(tc, q, k, x, Wv, out):
         def quant_w(b):
             wq[b] = work.tile([P, 512], U32, name="wq", tag="wq", align_bytes=64)
             ws[b] = work.tile([P, 512], U8, name="ws", tag="ws", align_bytes=64)
-            nc.vector.quantize_mx(out=wq[b][:].bitcast(FP8X4), scales=ws[b][:], in_=gw[b % 2][:])
+            nc.vector.quantize_mx(out=wq[b][:].bitcast(FP8X4), scales=ws[b][:], in_=gw[:])
 
         def values(b):
             v_ps = psum.tile([P, 4, H], F32, name="v_ps", tag="v")
@@ -213,27 +246,40 @@ def tile_retentionhead_pa_t_kernel(tc, q, k, x, Wv, out):
             return 0 <= b < B
 
         for i in range(-2, B + 1):
+            first = i == 0
             if on(i - 1):
                 outputs(i - 1)
-            if on(i):
+            if on(i) and not first:
                 values(i)
+            if on(i):
                 weigh(i, 3)
             if on(i + 1):
                 scores(i + 1, (3,))
+            if first:
+                weigh(0, 2)
+                weigh(0, 1)
+                quant_x(0)
+                values(0)
             if on(i + 2):
                 if (i + 2) % 2 == 0 and (i + 2) // 2 + AHEAD < B // 2 and (i + 2) // 2 > 0:
                     load_pair((i + 2) // 2 + AHEAD)
-                transposes(i + 2)
-            if on(i):
-                weigh(i, 2)
-                weigh(i, 0)
+                transposes_qk(i + 2)
             if on(i + 1):
-                scores(i + 1, (2, 0))
-            if on(i):
+                scores0(i + 1)
+            if on(i + 2):
+                transposes_x(i + 2)
+            if on(i) and not first:
+                weigh(i, 2)
+            if on(i + 1):
+                scores(i + 1, (2,))
+            if on(i) and not first:
                 weigh(i, 1)
             if on(i + 1):
                 scores(i + 1, (1,))
-                quant_x(i + 1)
+                if i + 1 > 0:
+                    quant_x(i + 1)
             if on(i):
                 quant_v(i)
                 quant_w(i)
+            if on(i + 1):
+                weigh0(i + 1)

@@ -27,7 +27,7 @@ def tile_retentionhead_pa_t_kernel(tc, q, k, x, Wv, out):
     with ExitStack() as ctx:
         const = ctx.enter_context(tc.tile_pool(name="const", bufs=1))
         loads = ctx.enter_context(tc.tile_pool(name="loads", bufs=AHEAD + 2))
-        work = ctx.enter_context(tc.tile_pool(name="work", bufs=2))
+        work = ctx.enter_context(tc.tile_pool(name="work", bufs=3))
         outs = ctx.enter_context(tc.tile_pool(name="outs", bufs=3))
         psum = ctx.enter_context(tc.psum_pool(name="psum", bufs=1))
         if PIN:
@@ -35,10 +35,9 @@ def tile_retentionhead_pa_t_kernel(tc, q, k, x, Wv, out):
 
         x_in, q_in, k_in = {}, {}, {}
 
-        def load_pair(g):
+        def load_qk(g):
             kt = loads.tile([P, 2 * 512], BF16, name="kt", tag="kt")
             qt = loads.tile([P, 2 * 512], BF16, name="qt", tag="qt")
-            xt = loads.tile([P, 2 * 2048], BF16, name="xt", tag="xt")
             bs = slice(2 * g, 2 * g + 2)
             nc.sync.dma_start(
                 out=kt[:].rearrange("p (b t h) -> p b t h", b=2, t=4),
@@ -48,26 +47,32 @@ def tile_retentionhead_pa_t_kernel(tc, q, k, x, Wv, out):
                 out=qt[:].rearrange("p (b w) -> p b w", b=2),
                 in_=q[bs].rearrange("b (p j) h -> p b (j h)", j=4),
             )
-            if g == 0:
+            k_in[g], q_in[g] = kt, qt
+
+        def load_x(g, split):
+            xt = loads.tile([P, 2 * 2048], BF16, name="xt", tag="xt")
+            x_in[g] = xt
+            if split:
                 for r in range(2):
                     nc.sync.dma_start(
-                        out=xt[:, r * 2048 : (r + 1) * 2048], in_=x[r].rearrange("(p j) c -> p (j c)", j=4)
+                        out=xt[:, r * 2048 : (r + 1) * 2048],
+                        in_=x[2 * g + r].rearrange("(p j) c -> p (j c)", j=4),
                     )
+                    if g == 0 and r == 0:
+                        nc.sync.dma_start(
+                            out=wv_sb[:].rearrange("q (u e) h -> q u e h", u=2),
+                            in_=Wv.rearrange("(u q e) h -> q u e h", u=2, e=2),
+                        )
             else:
                 nc.sync.dma_start(
                     out=xt[:].rearrange("p (b w) -> p b w", b=2),
-                    in_=x[bs].rearrange("b (p j) c -> p b (j c)", j=4),
+                    in_=x[2 * g : 2 * g + 2].rearrange("b (p j) c -> p b (j c)", j=4),
                 )
-            k_in[g], q_in[g], x_in[g] = kt, qt, xt
 
-        load_pair(0)
         wv_sb = const.tile([P, 4, H], BF16, name="wv_sb")
-        nc.sync.dma_start(
-            out=wv_sb[:].rearrange("q (u e) h -> q u e h", u=2),
-            in_=Wv.rearrange("(u q e) h -> q u e h", u=2, e=2),
-        )
-        for g in range(1, AHEAD + 1):
-            load_pair(g)
+        for g in range(AHEAD + 1):
+            load_qk(g)
+            load_x(g, g < 2)
 
         warm_in = const.tile([P, 1], F32, name="warm_in")
         warm_out = const.tile([P, 1], F32, name="warm_out")
@@ -168,7 +173,7 @@ def tile_retentionhead_pa_t_kernel(tc, q, k, x, Wv, out):
                     )
 
         def scores0(b):
-            s0_ps = psum.tile([P, P], F32, name="s0_ps", tag="o")
+            s0_ps = psum.tile([P, P], F32, name="s0_ps", tag="v")
             nc.tensor.matmul(
                 out=s0_ps[:].rearrange("p (j i) -> p j i", j=4),
                 lhsT=qkT[b][:, 0, :],
@@ -245,41 +250,55 @@ def tile_retentionhead_pa_t_kernel(tc, q, k, x, Wv, out):
         def on(b):
             return 0 <= b < B
 
-        for i in range(-2, B + 1):
-            first = i == 0
-            if on(i - 1):
+        nxt = {"tx": 0, "qx": 0, "val": 0, "qv": 0}
+
+        def tx_with_loads(b):
+            g = b // 2 + AHEAD
+            if b % 2 == 0 and b > 0 and g < B // 2:
+                load_qk(g)
+                load_x(g, False)
+            transposes_x(b)
+
+        def upto(kind, stage, target):
+            while nxt[kind] <= min(target, B - 1):
+                stage(nxt[kind])
+                nxt[kind] += 1
+
+        transposes_qk(0)
+        scores(0, (3, 2, 1))
+        scores0(0)
+        weigh0(0)
+        upto("tx", tx_with_loads, 0)
+        transposes_qk(1)
+        upto("tx", tx_with_loads, 1)
+
+        for i in range(0, B + 1):
+            if i > 0:
+                upto("val", values, nxt["qx"] - 1)
                 outputs(i - 1)
-            if on(i) and not first:
-                values(i)
             if on(i):
                 weigh(i, 3)
             if on(i + 1):
                 scores(i + 1, (3,))
-            if first:
-                weigh(0, 2)
-                weigh(0, 1)
-                quant_x(0)
-                values(0)
             if on(i + 2):
-                if (i + 2) % 2 == 0 and (i + 2) // 2 + AHEAD < B // 2 and (i + 2) // 2 > 0:
-                    load_pair((i + 2) // 2 + AHEAD)
                 transposes_qk(i + 2)
             if on(i + 1):
                 scores0(i + 1)
-            if on(i + 2):
-                transposes_x(i + 2)
-            if on(i) and not first:
+            upto("tx", tx_with_loads, i + 2 if i < 2 else i + 3)
+            if on(i):
                 weigh(i, 2)
             if on(i + 1):
                 scores(i + 1, (2,))
-            if on(i) and not first:
+            if on(i):
                 weigh(i, 1)
             if on(i + 1):
                 scores(i + 1, (1,))
-                if i + 1 > 0:
-                    quant_x(i + 1)
+            if i == 0:
+                upto("qx", quant_x, 0)
+                upto("val", values, 0)
+            upto("qx", quant_x, i + 1 if i < 3 else i + 2)
             if on(i):
-                quant_v(i)
                 quant_w(i)
+            upto("qv", quant_v, nxt["val"] - 1)
             if on(i + 1):
                 weigh0(i + 1)

@@ -40,8 +40,8 @@ def tile_retentionhead_pa_t_kernel(tc, q, k, x, Wv, out):
             qt = loads.tile([P, 2 * 512], BF16, name="qt", tag="qt")
             bs = slice(2 * g, 2 * g + 2)
             nc.sync.dma_start(
-                out=kt[:].rearrange("p (b t h) -> p b t h", b=2, t=4),
-                in_=k[bs].rearrange("b (t p) h -> p b t h", p=P),
+                out=kt[:].rearrange("p (b w) -> p b w", b=2),
+                in_=k[bs].rearrange("b (p j) h -> p b (j h)", j=4),
             )
             nc.sync.dma_start(
                 out=qt[:].rearrange("p (b w) -> p b w", b=2),
@@ -78,8 +78,10 @@ def tile_retentionhead_pa_t_kernel(tc, q, k, x, Wv, out):
         warm_out = const.tile([P, 1], F32, name="warm_out")
         nc.vector.memset(warm_in[:], 0.0)
         nc.scalar.activation(out=warm_out[:], in_=warm_in[:], func=ACT.Exp)
-        d_int = const.tile([P, P], I32, name="d_int")
-        nc.gpsimd.iota(out=d_int[:], pattern=[[1, 4], [4, 32]], base=0, channel_multiplier=-1)
+        part = const.tile([P, 1], I32, name="part")
+        nc.gpsimd.iota(out=part[:], pattern=[[0, 1]], base=0, channel_multiplier=1)
+        w_int = const.tile([P, P], I32, name="w_int")
+        nc.gpsimd.iota(out=w_int[:], pattern=[[1, 4], [4, 32]], base=0, channel_multiplier=0)
         ident_b = const.tile([P, P], BF16, name="ident_b")
         make_identity(nc, ident_b[:])
         ident_f = const.tile([P, P], F32, name="ident_f")
@@ -88,8 +90,18 @@ def tile_retentionhead_pa_t_kernel(tc, q, k, x, Wv, out):
         off4 = const.tile([P, 4], F32, name="off4")
         for s in range(4):
             nc.vector.memset(off4[:, s : s + 1], 128.0 * (3 - s))
+        key_lo = const.tile([P, 1], I32, name="key_lo")
+        nc.vector.tensor_scalar(
+            out=key_lo[:], in0=part[:], scalar1=31, scalar2=2, op0=ALU.bitwise_and, op1=ALU.logical_shift_left
+        )
+        key_hi = const.tile([P, 1], I32, name="key_hi")
+        nc.vector.tensor_scalar(out=key_hi[:], in0=part[:], scalar1=5, scalar2=None, op0=ALU.logical_shift_right)
+        key_int = const.tile([P, 1], I32, name="key_int")
+        nc.vector.tensor_tensor(out=key_int[:], in0=key_lo[:], in1=key_hi[:], op=ALU.bitwise_or)
+        key_f = const.tile([P, 1], F32, name="key_f")
+        nc.vector.tensor_copy(out=key_f[:], in_=key_int[:])
         d_f = const.tile([P, P], F32, name="d_f")
-        nc.vector.tensor_copy(out=d_f[:], in_=d_int[:])
+        nc.vector.tensor_scalar(out=d_f[:], in0=w_int[:], scalar1=key_f[:, 0:1], scalar2=None, op0=ALU.subtract)
         dist = const.tile([P, 1280], F32, name="dist")
         powers = const.tile([P, 1280], F32, name="powers")
         mask = const.tile([P, 1280], F32, name="mask")
@@ -124,30 +136,33 @@ def tile_retentionhead_pa_t_kernel(tc, q, k, x, Wv, out):
 
         def transposes_qk(b):
             g, r = divmod(b, 2)
-            qk_ps = psum.tile([P, 8, P], BF16, name="qk_ps", tag="qk")
-            for t in range(4):
-                nc.tensor.transpose(
-                    out=qk_ps[:, t, :], in_=k_in[g][:, r * 512 + t * P : r * 512 + (t + 1) * P], identity=ident_b[:]
-                )
+            qk_ps = psum.tile([P, 8 * P], BF16, name="qk_ps", tag="qk")
             for j in range(4):
+                cols = slice(r * 512 + j * P, r * 512 + (j + 1) * P)
+                nc.tensor.transpose(out=qk_ps[:, 2 * j * P : (2 * j + 1) * P], in_=k_in[g][:, cols], identity=ident_b[:])
                 nc.tensor.transpose(
-                    out=qk_ps[:, 4 + j, :], in_=q_in[g][:, r * 512 + j * P : r * 512 + (j + 1) * P], identity=ident_b[:]
+                    out=qk_ps[:, (2 * j + 1) * P : (2 * j + 2) * P], in_=q_in[g][:, cols], identity=ident_b[:]
                 )
             qkT[b] = work.tile([P, 8, P], BF16, name="qkT", tag="qkT")
-            nc.scalar.copy(out=qkT[b][:], in_=qk_ps[:])
+            nc.scalar.copy(
+                out=qkT[b][:].rearrange("h g (j r) -> h g j r", j=4),
+                in_=qk_ps[:].rearrange("h (j g r) -> h g j r", j=4, g=8),
+            )
 
         def transposes_x(b):
             g, r = divmod(b, 2)
             xw = x_in[g][:].bitcast(F32)
             gx[b] = work.tile([P, 2048], BF16, name="gx", tag="gx", align_bytes=64)
-            gxw = gx[b][:].bitcast(F32).rearrange("c (p hf s) -> c hf p s", hf=2, s=4)
+            gxw = gx[b][:].bitcast(F32).rearrange("c (t j r u) -> c j t r u", t=4, j=4, u=2)
             for hf in range(2):
                 x_ps = psum.tile([P, 4, P], F32, name="x_ps%d" % hf, tag="x%d" % hf)
                 for s in range(4):
                     j, u = 2 * hf + s // 2, s % 2
                     o = r * 1024 + j * 256 + u * P
                     nc.tensor.transpose(out=x_ps[:, s, :], in_=xw[:, o : o + P], identity=ident_f[:])
-                nc.scalar.copy(out=gxw[:, hf], in_=x_ps[:].rearrange("c s p -> c p s"))
+                nc.scalar.copy(
+                    out=gxw[:, 2 * hf : 2 * hf + 2], in_=x_ps[:].rearrange("c (j u) (t r) -> c j t r u", u=2, t=4)
+                )
 
         def quant_x(b):
             xq[b] = work.tile([P, 512], U32, name="xq", tag="xq", align_bytes=64)
@@ -165,9 +180,9 @@ def tile_retentionhead_pa_t_kernel(tc, q, k, x, Wv, out):
                 bank = s_ps[(b, tag)]
                 for t in range(jn + 1):
                     nc.tensor.matmul(
-                        out=bank[:, first + t, :].rearrange("p (j i) -> p j i", j=4),
+                        out=bank[:, first + t, :],
                         lhsT=qkT[b][:, t, :],
-                        rhs=qkT[b][:, 4:8, 32 * jn : 32 * jn + 32],
+                        rhs=qkT[b][:, 4 + jn, :],
                         start=True,
                         stop=True,
                     )
@@ -175,9 +190,9 @@ def tile_retentionhead_pa_t_kernel(tc, q, k, x, Wv, out):
         def scores0(b):
             s0_ps = psum.tile([P, P], F32, name="s0_ps", tag="v")
             nc.tensor.matmul(
-                out=s0_ps[:].rearrange("p (j i) -> p j i", j=4),
+                out=s0_ps[:],
                 lhsT=qkT[b][:, 0, :],
-                rhs=qkT[b][:, 4:8, 0:32],
+                rhs=qkT[b][:, 4, :],
                 start=True,
                 stop=True,
             )
@@ -297,8 +312,10 @@ def tile_retentionhead_pa_t_kernel(tc, q, k, x, Wv, out):
                 upto("qx", quant_x, 0)
                 upto("val", values, 0)
             upto("qx", quant_x, i + 1 if i < 3 else i + 2)
-            if on(i):
+            if i == 0:
                 quant_w(i)
             upto("qv", quant_v, nxt["val"] - 1)
+            if on(i) and i > 0:
+                quant_w(i)
             if on(i + 1):
                 weigh0(i + 1)

@@ -39,21 +39,32 @@ def tile_retentionhead_pa_t_kernel(tc, q, k, x, Wv, out):
             kt = loads.tile([P, 2 * 512], BF16, name="kt", tag="kt")
             qt = loads.tile([P, 2 * 512], BF16, name="qt", tag="qt")
             bs = slice(2 * g, 2 * g + 2)
+            k_in[g], q_in[g] = kt, qt
+            if g == 0:
+                return
             nc.sync.dma_start(
-                out=kt[:].rearrange("p (b w) -> p b w", b=2),
-                in_=k[bs].rearrange("b (p j) h -> p b (j h)", j=4),
+                out=kt[:].rearrange("p (b t h) -> p b t h", b=2, t=4),
+                in_=k[bs].rearrange("b (t p) h -> p b t h", p=P),
             )
             nc.sync.dma_start(
                 out=qt[:].rearrange("p (b w) -> p b w", b=2),
                 in_=q[bs].rearrange("b (p j) h -> p b (j h)", j=4),
             )
-            k_in[g], q_in[g] = kt, qt
+
+        def load_qk_one(r):
+            cols = slice(r * 512, (r + 1) * 512)
+            nc.sync.dma_start(
+                out=k_in[0][:, cols].rearrange("p (t h) -> p t h", t=4), in_=k[r].rearrange("(t p) h -> p t h", p=P)
+            )
+            nc.sync.dma_start(out=q_in[0][:, cols], in_=q[r].rearrange("(p j) h -> p (j h)", j=4))
 
         def load_x(g, split):
             xt = loads.tile([P, 2 * 2048], BF16, name="xt", tag="xt")
             x_in[g] = xt
             if split:
                 for r in range(2):
+                    if g == 0:
+                        load_qk_one(r)
                     nc.sync.dma_start(
                         out=xt[:, r * 2048 : (r + 1) * 2048],
                         in_=x[2 * g + r].rearrange("(p j) c -> p (j c)", j=4),
@@ -78,10 +89,8 @@ def tile_retentionhead_pa_t_kernel(tc, q, k, x, Wv, out):
         warm_out = const.tile([P, 1], F32, name="warm_out")
         nc.vector.memset(warm_in[:], 0.0)
         nc.scalar.activation(out=warm_out[:], in_=warm_in[:], func=ACT.Exp)
-        part = const.tile([P, 1], I32, name="part")
-        nc.gpsimd.iota(out=part[:], pattern=[[0, 1]], base=0, channel_multiplier=1)
-        w_int = const.tile([P, P], I32, name="w_int")
-        nc.gpsimd.iota(out=w_int[:], pattern=[[1, 4], [4, 32]], base=0, channel_multiplier=0)
+        d_int = const.tile([P, P], I32, name="d_int")
+        nc.gpsimd.iota(out=d_int[:], pattern=[[1, 4], [4, 32]], base=0, channel_multiplier=-1)
         ident_b = const.tile([P, P], BF16, name="ident_b")
         make_identity(nc, ident_b[:])
         ident_f = const.tile([P, P], F32, name="ident_f")
@@ -90,21 +99,10 @@ def tile_retentionhead_pa_t_kernel(tc, q, k, x, Wv, out):
         off4 = const.tile([P, 4], F32, name="off4")
         for s in range(4):
             nc.vector.memset(off4[:, s : s + 1], 128.0 * (3 - s))
-        key_lo = const.tile([P, 1], I32, name="key_lo")
-        nc.vector.tensor_scalar(
-            out=key_lo[:], in0=part[:], scalar1=31, scalar2=2, op0=ALU.bitwise_and, op1=ALU.logical_shift_left
-        )
-        key_hi = const.tile([P, 1], I32, name="key_hi")
-        nc.vector.tensor_scalar(out=key_hi[:], in0=part[:], scalar1=5, scalar2=None, op0=ALU.logical_shift_right)
-        key_int = const.tile([P, 1], I32, name="key_int")
-        nc.vector.tensor_tensor(out=key_int[:], in0=key_lo[:], in1=key_hi[:], op=ALU.bitwise_or)
-        key_f = const.tile([P, 1], F32, name="key_f")
-        nc.vector.tensor_copy(out=key_f[:], in_=key_int[:])
         d_f = const.tile([P, P], F32, name="d_f")
-        nc.vector.tensor_scalar(out=d_f[:], in0=w_int[:], scalar1=key_f[:, 0:1], scalar2=None, op0=ALU.subtract)
+        nc.vector.tensor_copy(out=d_f[:], in_=d_int[:])
         dist = const.tile([P, 1280], F32, name="dist")
         powers = const.tile([P, 1280], F32, name="powers")
-        mask = const.tile([P, 1280], F32, name="mask")
         tab = const.tile([P, 1280], F32, name="tab")
         gw = const.tile([P, 2048], BF16, name="gw", align_bytes=64)
         for jn in (3, 2, 1, 0):
@@ -116,13 +114,15 @@ def tile_retentionhead_pa_t_kernel(tc, q, k, x, Wv, out):
                 in1=off4[:, 3 - jn : 4].unsqueeze(1).to_broadcast([P, P, n]),
                 op=ALU.add,
             )
-            nc.scalar.activation(out=powers[:, sl], in_=dist[:, sl], func=ACT.Exp, scale=math.log(GAMMA))
-            nc.vector.tensor_scalar(
-                out=mask[:, sl], in0=dist[:, sl], scalar1=0.0, scalar2=C**-0.5, op0=ALU.is_ge, op1=ALU.mult
+            nc.scalar.activation(
+                out=powers[:, sl], in_=dist[:, sl], func=ACT.Exp, scale=math.log(GAMMA), bias=-0.5 * math.log(C)
             )
-            if jn == 3:
-                nc.vector.memset(gw[:].bitcast(I32), 0)
-            nc.vector.tensor_tensor(out=tab[:, sl], in0=powers[:, sl], in1=mask[:, sl], op=ALU.mult)
+        nc.vector.memset(gw[:].bitcast(I32), 0)
+        for jn in (3, 2, 1, 0):
+            sl = slice(TAB_OFF[jn], TAB_OFF[jn] + P * (jn + 1))
+            nc.vector.scalar_tensor_tensor(
+                out=tab[:, sl], in0=dist[:, sl], scalar=0.0, in1=powers[:, sl], op0=ALU.is_ge, op1=ALU.mult
+            )
 
         g_wv = const.tile([P, H, 4], BF16, name="g_wv", align_bytes=64)
         nc.vector.tensor_copy(out=g_wv[:], in_=wv_sb[:].rearrange("q t h -> q h t"))
@@ -136,40 +136,37 @@ def tile_retentionhead_pa_t_kernel(tc, q, k, x, Wv, out):
 
         def transposes_qk(b):
             g, r = divmod(b, 2)
-            qk_ps = psum.tile([P, 8 * P], BF16, name="qk_ps", tag="qk")
-            for j in range(4):
-                cols = slice(r * 512 + j * P, r * 512 + (j + 1) * P)
-                nc.tensor.transpose(out=qk_ps[:, 2 * j * P : (2 * j + 1) * P], in_=k_in[g][:, cols], identity=ident_b[:])
+            qk_ps = psum.tile([P, 8, P], BF16, name="qk_ps", tag="qk")
+            for t in range(4):
                 nc.tensor.transpose(
-                    out=qk_ps[:, (2 * j + 1) * P : (2 * j + 2) * P], in_=q_in[g][:, cols], identity=ident_b[:]
+                    out=qk_ps[:, t, :], in_=k_in[g][:, r * 512 + t * P : r * 512 + (t + 1) * P], identity=ident_b[:]
+                )
+            for j in range(4):
+                nc.tensor.transpose(
+                    out=qk_ps[:, 4 + j, :], in_=q_in[g][:, r * 512 + j * P : r * 512 + (j + 1) * P], identity=ident_b[:]
                 )
             qkT[b] = work.tile([P, 8, P], BF16, name="qkT", tag="qkT")
-            nc.scalar.copy(
-                out=qkT[b][:].rearrange("h g (j r) -> h g j r", j=4),
-                in_=qk_ps[:].rearrange("h (j g r) -> h g j r", j=4, g=8),
-            )
+            nc.scalar.copy(out=qkT[b][:], in_=qk_ps[:])
 
         def transposes_x(b):
             g, r = divmod(b, 2)
             xw = x_in[g][:].bitcast(F32)
             gx[b] = work.tile([P, 2048], BF16, name="gx", tag="gx", align_bytes=64)
-            gxw = gx[b][:].bitcast(F32).rearrange("c (t j r u) -> c j t r u", t=4, j=4, u=2)
+            gxw = gx[b][:].bitcast(F32).rearrange("c (p hf s) -> c hf p s", hf=2, s=4)
             for hf in range(2):
                 x_ps = psum.tile([P, 4, P], F32, name="x_ps%d" % hf, tag="x%d" % hf)
                 for s in range(4):
                     j, u = 2 * hf + s // 2, s % 2
                     o = r * 1024 + j * 256 + u * P
                     nc.tensor.transpose(out=x_ps[:, s, :], in_=xw[:, o : o + P], identity=ident_f[:])
-                nc.scalar.copy(
-                    out=gxw[:, 2 * hf : 2 * hf + 2], in_=x_ps[:].rearrange("c (j u) (t r) -> c j t r u", u=2, t=4)
-                )
+                nc.scalar.copy(out=gxw[:, hf], in_=x_ps[:].rearrange("c s p -> c p s"))
 
         def quant_x(b):
             xq[b] = work.tile([P, 512], U32, name="xq", tag="xq", align_bytes=64)
             xs[b] = work.tile([P, 512], U8, name="xs", tag="xs", align_bytes=64)
             nc.vector.quantize_mx(out=xq[b][:].bitcast(FP8X4), scales=xs[b][:], in_=gx[b][:])
 
-        S_SLOT = {3: ("sa", 0), 2: ("sb", 0), 1: ("sc", 0)}
+        S_SLOT = {3: ("sa", 0), 2: ("sb", 0), 1: ("sc", 0), 0: ("sc", 2)}
         s0_sb = {}
 
         def scores(b, jns):
@@ -180,26 +177,16 @@ def tile_retentionhead_pa_t_kernel(tc, q, k, x, Wv, out):
                 bank = s_ps[(b, tag)]
                 for t in range(jn + 1):
                     nc.tensor.matmul(
-                        out=bank[:, first + t, :],
+                        out=bank[:, first + t, :].rearrange("p (j i) -> p j i", j=4),
                         lhsT=qkT[b][:, t, :],
-                        rhs=qkT[b][:, 4 + jn, :],
+                        rhs=qkT[b][:, 4:8, 32 * jn : 32 * jn + 32],
                         start=True,
                         stop=True,
                     )
 
-        def scores0(b):
-            s0_ps = psum.tile([P, P], F32, name="s0_ps", tag="v")
-            nc.tensor.matmul(
-                out=s0_ps[:],
-                lhsT=qkT[b][:, 0, :],
-                rhs=qkT[b][:, 4, :],
-                start=True,
-                stop=True,
-            )
-            s0_sb[b] = work.tile([P, P], F32, name="s0_sb", tag="s0_sb")
-            nc.scalar.copy(out=s0_sb[b][:], in_=s0_ps[:])
-
         def weigh0(b):
+            s0_sb[b] = work.tile([P, P], F32, name="s0_sb", tag="s0_sb")
+            nc.vector.tensor_copy(out=s0_sb[b][:], in_=s_ps[(b, "sc")][:, 2, :])
             nc.gpsimd.tensor_tensor(
                 out=gw[:].rearrange("p (j i t) -> p j i t", j=4, t=4)[:, :, 0:32, 0:1],
                 in0=s0_sb[b][:].rearrange("p (j i t) -> p j i t", j=4, t=1),
@@ -280,9 +267,7 @@ def tile_retentionhead_pa_t_kernel(tc, q, k, x, Wv, out):
                 nxt[kind] += 1
 
         transposes_qk(0)
-        scores(0, (3, 2, 1))
-        scores0(0)
-        weigh0(0)
+        scores(0, (3, 2, 1, 0))
         upto("tx", tx_with_loads, 0)
         transposes_qk(1)
         upto("tx", tx_with_loads, 1)
@@ -291,31 +276,31 @@ def tile_retentionhead_pa_t_kernel(tc, q, k, x, Wv, out):
             if i > 0:
                 upto("val", values, nxt["qx"] - 1)
                 outputs(i - 1)
-            if on(i):
-                weigh(i, 3)
-            if on(i + 1):
-                scores(i + 1, (3,))
             if on(i + 2):
                 transposes_qk(i + 2)
-            if on(i + 1):
-                scores0(i + 1)
-            upto("tx", tx_with_loads, i + 2 if i < 2 else i + 3)
             if on(i):
+                weigh0(i)
+                weigh(i, 3)
+            if i == 0:
+                weigh(i, 2)
+                weigh(i, 1)
+                upto("qx", quant_x, 0)
+            if on(i + 1):
+                scores(i + 1, (3,))
+            if i == 0:
+                upto("val", values, 0)
+            upto("tx", tx_with_loads, i + 2 if i < 2 else i + 3)
+            if on(i) and i > 0:
                 weigh(i, 2)
             if on(i + 1):
                 scores(i + 1, (2,))
-            if on(i):
+            if on(i) and i > 0:
                 weigh(i, 1)
             if on(i + 1):
-                scores(i + 1, (1,))
-            if i == 0:
-                upto("qx", quant_x, 0)
-                upto("val", values, 0)
-            upto("qx", quant_x, i + 1 if i < 3 else i + 2)
+                scores(i + 1, (1, 0))
             if i == 0:
                 quant_w(i)
-            upto("qv", quant_v, nxt["val"] - 1)
+            upto("qx", quant_x, i + 1 if i < 3 else i + 2)
             if on(i) and i > 0:
                 quant_w(i)
-            if on(i + 1):
-                weigh0(i + 1)
+            upto("qv", quant_v, nxt["val"] - 1)

@@ -18,6 +18,7 @@ P = 128
 GAMMA = 0.96875
 FLOPS = 3 * 2 * B * T * T * H
 PIN = True
+BUFS = 2
 AHEAD = 2
 TAB_OFF = (0, 128, 384, 768)
 
@@ -85,6 +86,13 @@ def tile_retentionhead_pa_t_kernel(tc, q, k, x, Wv, out):
             load_qk(g)
             load_x(g, g < 2)
 
+        zeros = const.tile([P, 512], BF16, name="zeros")
+        nc.vector.memset(zeros[:].bitcast(I32), 0)
+        idle = psum.tile([P, 4, P], F32, name="idle", tag="sa")
+        for n in range(4):
+            nc.tensor.matmul(
+                out=idle[:].rearrange("p t n -> p (t n)"), lhsT=zeros[:, 0:P], rhs=zeros[:], start=True, stop=True
+            )
         warm_in = const.tile([P, 1], F32, name="warm_in")
         warm_out = const.tile([P, 1], F32, name="warm_out")
         nc.vector.memset(warm_in[:], 0.0)
@@ -96,6 +104,9 @@ def tile_retentionhead_pa_t_kernel(tc, q, k, x, Wv, out):
         ident_f = const.tile([P, P], F32, name="ident_f")
         make_identity(nc, ident_f[:])
 
+        gwx = [const.tile([P, 4096], BF16, name="gwx%d" % n, align_bytes=64) for n in range(BUFS)]
+        nc.gpsimd.memset(gwx[1][:, 0:2048].bitcast(I32), 0)
+
         off4 = const.tile([P, 4], F32, name="off4")
         for s in range(4):
             nc.vector.memset(off4[:, s : s + 1], 128.0 * (3 - s))
@@ -104,7 +115,6 @@ def tile_retentionhead_pa_t_kernel(tc, q, k, x, Wv, out):
         dist = const.tile([P, 1280], F32, name="dist")
         powers = const.tile([P, 1280], F32, name="powers")
         tab = const.tile([P, 1280], F32, name="tab")
-        gw = const.tile([P, 2048], BF16, name="gw", align_bytes=64)
         for jn in (3, 2, 1, 0):
             n = jn + 1
             sl = slice(TAB_OFF[jn], TAB_OFF[jn] + P * n)
@@ -117,7 +127,7 @@ def tile_retentionhead_pa_t_kernel(tc, q, k, x, Wv, out):
             nc.scalar.activation(
                 out=powers[:, sl], in_=dist[:, sl], func=ACT.Exp, scale=math.log(GAMMA), bias=-0.5 * math.log(C)
             )
-        nc.vector.memset(gw[:].bitcast(I32), 0)
+        nc.vector.memset(gwx[0][:, 0:2048].bitcast(I32), 0)
         for jn in (3, 2, 1, 0):
             sl = slice(TAB_OFF[jn], TAB_OFF[jn] + P * (jn + 1))
             nc.vector.scalar_tensor_tensor(
@@ -132,7 +142,10 @@ def tile_retentionhead_pa_t_kernel(tc, q, k, x, Wv, out):
             out=wv_q[:].bitcast(FP8X4), scales=wv_s[:], in_=g_wv[:].rearrange("q h t -> q (h t)")
         )
 
-        qkT, gx, xq, xs, gv, vq, vs, wq, ws, s_ps = {}, {}, {}, {}, {}, {}, {}, {}, {}, {}
+        def on(b):
+            return 0 <= b < B
+
+        qkT, xq, xs, gv, vq, vs, wq, ws, s_ps = {}, {}, {}, {}, {}, {}, {}, {}, {}
 
         def transposes_qk(b):
             g, r = divmod(b, 2)
@@ -151,20 +164,26 @@ def tile_retentionhead_pa_t_kernel(tc, q, k, x, Wv, out):
         def transposes_x(b):
             g, r = divmod(b, 2)
             xw = x_in[g][:].bitcast(F32)
-            gx[b] = work.tile([P, 2048], BF16, name="gx", tag="gx", align_bytes=64)
-            gxw = gx[b][:].bitcast(F32).rearrange("c (p hf s) -> c hf p s", hf=2, s=4)
+            gx = gwx[(b - 2) % BUFS][:, 2048:4096]
+            gxw = gx.bitcast(F32).rearrange("c (p hf s) -> c hf p s", hf=2, s=4)
             for hf in range(2):
                 x_ps = psum.tile([P, 4, P], F32, name="x_ps%d" % hf, tag="x%d" % hf)
                 for s in range(4):
                     j, u = 2 * hf + s // 2, s % 2
                     o = r * 1024 + j * 256 + u * P
                     nc.tensor.transpose(out=x_ps[:, s, :], in_=xw[:, o : o + P], identity=ident_f[:])
-                nc.scalar.copy(out=gxw[:, hf], in_=x_ps[:].rearrange("c s p -> c p s"))
+                copy = nc.vector.tensor_copy if hf == 1 and b in (1, 2) else nc.scalar.copy
+                copy(out=gxw[:, hf], in_=x_ps[:].rearrange("c s p -> c p s"))
 
-        def quant_x(b):
-            xq[b] = work.tile([P, 512], U32, name="xq", tag="xq", align_bytes=64)
-            xs[b] = work.tile([P, 512], U8, name="xs", tag="xs", align_bytes=64)
-            nc.vector.quantize_mx(out=xq[b][:].bitcast(FP8X4), scales=xs[b][:], in_=gx[b][:])
+        def quant_wx(i):
+            lo, hi = (0 if on(i) else 512), (1024 if on(i + 2) else 512)
+            codes = work.tile([P, 1024], U32, name="codes", tag="codes", align_bytes=64)
+            scales = work.tile([P, 1024], U8, name="scales", tag="scales", align_bytes=64)
+            nc.vector.quantize_mx(
+                out=codes[:, lo:hi].bitcast(FP8X4), scales=scales[:, lo:hi], in_=gwx[i % BUFS][:, 4 * lo : 4 * hi]
+            )
+            wq[i], ws[i] = codes[:, 0:512], scales[:, 0:512]
+            xq[i + 2], xs[i + 2] = codes[:, 512:1024], scales[:, 512:1024]
 
         S_SLOT = {3: ("sa", 0), 2: ("sb", 0), 1: ("sc", 0), 0: ("sc", 2)}
         s0_sb = {}
@@ -184,11 +203,17 @@ def tile_retentionhead_pa_t_kernel(tc, q, k, x, Wv, out):
                         stop=True,
                     )
 
-        def weigh0(b):
+        def copy0(b):
             s0_sb[b] = work.tile([P, P], F32, name="s0_sb", tag="s0_sb")
-            nc.vector.tensor_copy(out=s0_sb[b][:], in_=s_ps[(b, "sc")][:, 2, :])
+            copy = nc.vector.tensor_copy if b % 2 == 0 else nc.scalar.copy
+            copy(out=s0_sb[b][:], in_=s_ps[(b, "sc")][:, 2, :])
+
+        def weigh0(b):
+            if b % 2 == 1:
+                code = work.tile([P, 1], U32, name="code", tag="code")
+                nc.gpsimd.tensor_copy(out=code[:], in_=wq[b - 1][:, 0:1])
             nc.gpsimd.tensor_tensor(
-                out=gw[:].rearrange("p (j i t) -> p j i t", j=4, t=4)[:, :, 0:32, 0:1],
+                out=gwx[b % BUFS][:, 0:2048].rearrange("p (j i t) -> p j i t", j=4, t=4)[:, :, 0:32, 0:1],
                 in0=s0_sb[b][:].rearrange("p (j i t) -> p j i t", j=4, t=1),
                 in1=tab[:, 0:P].rearrange("p (j i t) -> p j i t", j=4, t=1),
                 op=ALU.mult,
@@ -198,16 +223,11 @@ def tile_retentionhead_pa_t_kernel(tc, q, k, x, Wv, out):
             tag, first = S_SLOT[jn]
             n = jn + 1
             nc.vector.tensor_tensor(
-                out=gw[:].rearrange("p (j i t) -> p j i t", j=4, t=4)[:, :, 32 * jn : 32 * jn + 32, 0:n],
+                out=gwx[b % BUFS][:, 0:2048].rearrange("p (j i t) -> p j i t", j=4, t=4)[:, :, 32 * jn : 32 * jn + 32, 0:n],
                 in0=s_ps[(b, tag)][:, first : first + n, :].rearrange("p t (j i) -> p j i t", j=4),
                 in1=tab[:, TAB_OFF[jn] : TAB_OFF[jn] + P * n].rearrange("p (j i t) -> p j i t", j=4, t=n),
                 op=ALU.mult,
             )
-
-        def quant_w(b):
-            wq[b] = work.tile([P, 512], U32, name="wq", tag="wq", align_bytes=64)
-            ws[b] = work.tile([P, 512], U8, name="ws", tag="ws", align_bytes=64)
-            nc.vector.quantize_mx(out=wq[b][:].bitcast(FP8X4), scales=ws[b][:], in_=gw[:])
 
         def values(b):
             v_ps = psum.tile([P, 4, H], F32, name="v_ps", tag="v")
@@ -233,11 +253,12 @@ def tile_retentionhead_pa_t_kernel(tc, q, k, x, Wv, out):
             )
 
         def outputs(b):
-            o_ps = psum.tile([P, 4, H], F32, name="o_ps", tag="o")
+            halves = [psum.tile([P, 4, H], F32, name="o_ps", tag="o")]
+            halves.append(psum.tile([P, 4, H], F32, name="v_ps", tag="v") if b == B - 1 else halves[0])
             for j in range(4):
                 cols = slice(j * P, (j + 1) * P)
                 nc.tensor.matmul_mx(
-                    out=o_ps[:, j, :],
+                    out=halves[j // 2][:, j, :],
                     lhsT=wq[b][:, cols].bitcast(FP8X4),
                     lhsT_scale=ws[b][:, cols],
                     rhs=vq[b][:].bitcast(FP8X4),
@@ -246,13 +267,16 @@ def tile_retentionhead_pa_t_kernel(tc, q, k, x, Wv, out):
                     stop=True,
                 )
             o_sb = outs.tile([P, 4, H], F32, name="o_sb", tag="o_sb")
-            nc.scalar.copy(out=o_sb[:], in_=o_ps[:])
-            nc.sync.dma_start(out=out[b].rearrange("(i j) h -> i j h", j=4), in_=o_sb[:])
-
-        def on(b):
-            return 0 <= b < B
-
-        nxt = {"tx": 0, "qx": 0, "val": 0, "qv": 0}
+            out_b = out[b].rearrange("(i j) h -> i j h", j=4)
+            if b < B - 1:
+                nc.scalar.copy(out=o_sb[:], in_=halves[0][:])
+                nc.sync.dma_start(out=out_b, in_=o_sb[:])
+            else:
+                o_sb2 = outs.tile([P, 2, H], F32, name="o_sb2", tag="o_sb2")
+                nc.scalar.copy(out=o_sb[:, 0:2, :], in_=halves[0][:, 0:2, :])
+                nc.vector.tensor_copy(out=o_sb2[:], in_=halves[1][:, 2:4, :])
+                nc.sync.dma_start(out=out_b[:, 0:2, :], in_=o_sb[:, 0:2, :])
+                nc.sync.dma_start(out=out_b[:, 2:4, :], in_=o_sb2[:])
 
         def tx_with_loads(b):
             g = b // 2 + AHEAD
@@ -261,46 +285,41 @@ def tile_retentionhead_pa_t_kernel(tc, q, k, x, Wv, out):
                 load_x(g, False)
             transposes_x(b)
 
-        def upto(kind, stage, target):
-            while nxt[kind] <= min(target, B - 1):
-                stage(nxt[kind])
-                nxt[kind] += 1
-
         transposes_qk(0)
+        tx_with_loads(0)
         scores(0, (3, 2, 1, 0))
-        upto("tx", tx_with_loads, 0)
         transposes_qk(1)
-        upto("tx", tx_with_loads, 1)
 
         for i in range(0, B + 1):
             if i > 0:
-                upto("val", values, nxt["qx"] - 1)
+                if on(i + 1):
+                    values(i + 1)
                 outputs(i - 1)
-            if on(i + 2):
-                transposes_qk(i + 2)
             if on(i):
+                if i == 0:
+                    quant_wx(-2)
+                if i % 2 == 0:
+                    copy0(i)
                 weigh0(i)
-                weigh(i, 3)
-            if i == 0:
-                weigh(i, 2)
-                weigh(i, 1)
-                upto("qx", quant_x, 0)
-            if on(i + 1):
-                scores(i + 1, (3,))
-            if i == 0:
-                upto("val", values, 0)
-            upto("tx", tx_with_loads, i + 2 if i < 2 else i + 3)
-            if on(i) and i > 0:
-                weigh(i, 2)
-            if on(i + 1):
-                scores(i + 1, (2,))
-            if on(i) and i > 0:
-                weigh(i, 1)
-            if on(i + 1):
-                scores(i + 1, (1, 0))
-            if i == 0:
-                quant_w(i)
-            upto("qx", quant_x, i + 1 if i < 3 else i + 2)
-            if on(i) and i > 0:
-                quant_w(i)
-            upto("qv", quant_v, nxt["val"] - 1)
+                if i == 0:
+                    for jn in (3, 2, 1):
+                        weigh(i, jn)
+                    tx_with_loads(1)
+                    values(0)
+                    quant_wx(-1)
+                for jn in (3, 2, 1):
+                    if i > 0:
+                        weigh(i, jn)
+                    if on(i + 1):
+                        scores(i + 1, (1, 0) if jn == 1 else (jn,))
+                if on(i + 1) and i % 2 == 0:
+                    copy0(i + 1)
+                if i == 0:
+                    tx_with_loads(2)
+                    values(1)
+                if on(i + 2):
+                    transposes_qk(i + 2)
+                if on(i + 3):
+                    tx_with_loads(i + 3)
+                quant_v(i)
+                quant_wx(i)

@@ -20,7 +20,6 @@ FLOPS = 3 * 2 * B * T * T * H
 PIN = True
 BUFS = 2
 AHEAD = 2
-TAB_OFF = (0, 128, 384, 768)
 
 
 def tile_retentionhead_pa_t_kernel(tc, q, k, x, Wv, out):
@@ -64,12 +63,12 @@ def tile_retentionhead_pa_t_kernel(tc, q, k, x, Wv, out):
             x_in[g] = xt
             if split:
                 for r in range(2):
-                    if g == 0:
-                        load_qk_one(r)
                     nc.sync.dma_start(
                         out=xt[:, r * 2048 : (r + 1) * 2048],
                         in_=x[2 * g + r].rearrange("(p j) c -> p (j c)", j=4),
                     )
+                    if g == 0:
+                        load_qk_one(r)
                     if g == 0 and r == 0:
                         nc.sync.dma_start(
                             out=wv_sb[:].rearrange("q (u e) h -> q u e h", u=2),
@@ -86,61 +85,57 @@ def tile_retentionhead_pa_t_kernel(tc, q, k, x, Wv, out):
             load_qk(g)
             load_x(g, g < 2)
 
-        zeros = const.tile([P, 512], BF16, name="zeros")
+        zeros = const.tile([P, P], BF16, name="zeros")
         nc.vector.memset(zeros[:].bitcast(I32), 0)
         idle = psum.tile([P, 4, P], F32, name="idle", tag="sa")
-        for n in range(4):
-            nc.tensor.matmul(
-                out=idle[:].rearrange("p t n -> p (t n)"), lhsT=zeros[:, 0:P], rhs=zeros[:], start=True, stop=True
-            )
+        for n in range(16):
+            nc.tensor.matmul(out=idle[:, n % 4, :], lhsT=zeros[:], rhs=zeros[:], start=True, stop=True)
         warm_in = const.tile([P, 1], F32, name="warm_in")
         warm_out = const.tile([P, 1], F32, name="warm_out")
         nc.vector.memset(warm_in[:], 0.0)
         nc.scalar.activation(out=warm_out[:], in_=warm_in[:], func=ACT.Exp)
-        d_int = const.tile([P, P], I32, name="d_int")
-        nc.gpsimd.iota(out=d_int[:], pattern=[[1, 4], [4, 32]], base=0, channel_multiplier=-1)
+        d_f = const.tile([P, P], F32, name="d_f")
+        nc.gpsimd.iota(
+            out=d_f[:], pattern=[[1, 4], [4, 32]], base=0, channel_multiplier=-1, allow_small_or_imprecise_dtypes=True
+        )
+        off4 = const.tile([P, 4], F32, name="off4")
+        nc.gpsimd.iota(
+            out=off4[:], pattern=[[-P, 4]], base=3 * P, channel_multiplier=0, allow_small_or_imprecise_dtypes=True
+        )
         ident_b = const.tile([P, P], BF16, name="ident_b")
         make_identity(nc, ident_b[:])
         ident_f = const.tile([P, P], F32, name="ident_f")
         make_identity(nc, ident_f[:])
-
         gwx = [const.tile([P, 4096], BF16, name="gwx%d" % n, align_bytes=64) for n in range(BUFS)]
-        nc.gpsimd.memset(gwx[1][:, 0:2048].bitcast(I32), 0)
+        for n in range(BUFS):
+            nc.gpsimd.memset(gwx[n][:, 0:2048].bitcast(I32), 0)
 
-        off4 = const.tile([P, 4], F32, name="off4")
-        for s in range(4):
-            nc.vector.memset(off4[:, s : s + 1], 128.0 * (3 - s))
-        d_f = const.tile([P, P], F32, name="d_f")
-        nc.vector.tensor_copy(out=d_f[:], in_=d_int[:])
-        dist = const.tile([P, 1280], F32, name="dist")
-        powers = const.tile([P, 1280], F32, name="powers")
-        tab = const.tile([P, 1280], F32, name="tab")
-        for jn in (3, 2, 1, 0):
-            n = jn + 1
-            sl = slice(TAB_OFF[jn], TAB_OFF[jn] + P * n)
-            nc.vector.tensor_tensor(
-                out=dist[:, sl].rearrange("p (w t) -> p w t", t=n),
-                in0=d_f[:].unsqueeze(2).to_broadcast([P, P, n]),
-                in1=off4[:, 3 - jn : 4].unsqueeze(1).to_broadcast([P, P, n]),
-                op=ALU.add,
-            )
-            nc.scalar.activation(
-                out=powers[:, sl], in_=dist[:, sl], func=ACT.Exp, scale=math.log(GAMMA), bias=-0.5 * math.log(C)
-            )
-        nc.vector.memset(gwx[0][:, 0:2048].bitcast(I32), 0)
-        for jn in (3, 2, 1, 0):
-            sl = slice(TAB_OFF[jn], TAB_OFF[jn] + P * (jn + 1))
-            nc.vector.scalar_tensor_tensor(
-                out=tab[:, sl], in0=dist[:, sl], scalar=0.0, in1=powers[:, sl], op0=ALU.is_ge, op1=ALU.mult
-            )
+        dist = const.tile([P, P, 4], F32, name="dist")
+        powers = const.tile([P, P, 4], F32, name="powers")
+        tab = [const.tile([P, P, jn + 1], F32, name="tab%d" % jn) for jn in range(4)]
+        nc.vector.tensor_tensor(
+            out=dist[:],
+            in0=d_f[:].unsqueeze(2).to_broadcast([P, P, 4]),
+            in1=off4[:].unsqueeze(1).to_broadcast([P, P, 4]),
+            op=ALU.add,
+        )
+        nc.scalar.activation(out=powers[:], in_=dist[:], func=ACT.Exp, scale=math.log(GAMMA), bias=-0.5 * math.log(C))
+        nc.vector.scalar_tensor_tensor(
+            out=tab[3][:], in0=dist[:], scalar=0.0, in1=powers[:], op0=ALU.is_ge, op1=ALU.mult
+        )
+        nc.scalar.copy(out=tab[0][:], in_=tab[3][:, :, 3:4])
+        nc.vector.tensor_copy(out=tab[2][:], in_=tab[3][:, :, 1:4])
+        nc.scalar.copy(out=tab[1][:], in_=tab[3][:, :, 2:4])
 
         g_wv = const.tile([P, H, 4], BF16, name="g_wv", align_bytes=64)
-        nc.vector.tensor_copy(out=g_wv[:], in_=wv_sb[:].rearrange("q t h -> q h t"))
         wv_q = const.tile([P, H], U32, name="wv_q", align_bytes=64)
         wv_s = const.tile([P, H], U8, name="wv_s", align_bytes=64)
-        nc.vector.quantize_mx(
-            out=wv_q[:].bitcast(FP8X4), scales=wv_s[:], in_=g_wv[:].rearrange("q h t -> q (h t)")
-        )
+
+        def quant_wv():
+            nc.vector.tensor_copy(out=g_wv[:], in_=wv_sb[:].rearrange("q t h -> q h t"))
+            nc.vector.quantize_mx(
+                out=wv_q[:].bitcast(FP8X4), scales=wv_s[:], in_=g_wv[:].rearrange("q h t -> q (h t)")
+            )
 
         def on(b):
             return 0 <= b < B
@@ -172,16 +167,21 @@ def tile_retentionhead_pa_t_kernel(tc, q, k, x, Wv, out):
                     j, u = 2 * hf + s // 2, s % 2
                     o = r * 1024 + j * 256 + u * P
                     nc.tensor.transpose(out=x_ps[:, s, :], in_=xw[:, o : o + P], identity=ident_f[:])
-                copy = nc.vector.tensor_copy if hf == 1 and b in (1, 2) else nc.scalar.copy
+                copy = nc.vector.tensor_copy if hf == 1 and b < 3 else nc.scalar.copy
                 copy(out=gxw[:, hf], in_=x_ps[:].rearrange("c s p -> c p s"))
 
         def quant_wx(i):
             lo, hi = (0 if on(i) else 512), (1024 if on(i + 2) else 512)
             codes = work.tile([P, 1024], U32, name="codes", tag="codes", align_bytes=64)
             scales = work.tile([P, 1024], U8, name="scales", tag="scales", align_bytes=64)
-            nc.vector.quantize_mx(
-                out=codes[:, lo:hi].bitcast(FP8X4), scales=scales[:, lo:hi], in_=gwx[i % BUFS][:, 4 * lo : 4 * hi]
-            )
+            step = 256 if i == B - 1 else hi - lo
+            for c in range(lo, hi, step):
+                cols = slice(c, c + step)
+                nc.vector.quantize_mx(
+                    out=codes[:, cols].bitcast(FP8X4),
+                    scales=scales[:, cols],
+                    in_=gwx[i % BUFS][:, 4 * c : 4 * (c + step)],
+                )
             wq[i], ws[i] = codes[:, 0:512], scales[:, 0:512]
             xq[i + 2], xs[i + 2] = codes[:, 512:1024], scales[:, 512:1024]
 
@@ -205,17 +205,16 @@ def tile_retentionhead_pa_t_kernel(tc, q, k, x, Wv, out):
 
         def copy0(b):
             s0_sb[b] = work.tile([P, P], F32, name="s0_sb", tag="s0_sb")
-            copy = nc.vector.tensor_copy if b % 2 == 0 else nc.scalar.copy
-            copy(out=s0_sb[b][:], in_=s_ps[(b, "sc")][:, 2, :])
+            nc.scalar.copy(out=s0_sb[b][:], in_=s_ps[(b, "sc")][:, 2, :])
 
         def weigh0(b):
-            if b % 2 == 1:
+            if on(b - 1):
                 code = work.tile([P, 1], U32, name="code", tag="code")
                 nc.gpsimd.tensor_copy(out=code[:], in_=wq[b - 1][:, 0:1])
             nc.gpsimd.tensor_tensor(
                 out=gwx[b % BUFS][:, 0:2048].rearrange("p (j i t) -> p j i t", j=4, t=4)[:, :, 0:32, 0:1],
                 in0=s0_sb[b][:].rearrange("p (j i t) -> p j i t", j=4, t=1),
-                in1=tab[:, 0:P].rearrange("p (j i t) -> p j i t", j=4, t=1),
+                in1=tab[0][:].rearrange("p (j i) t -> p j i t", j=4),
                 op=ALU.mult,
             )
 
@@ -225,7 +224,7 @@ def tile_retentionhead_pa_t_kernel(tc, q, k, x, Wv, out):
             nc.vector.tensor_tensor(
                 out=gwx[b % BUFS][:, 0:2048].rearrange("p (j i t) -> p j i t", j=4, t=4)[:, :, 32 * jn : 32 * jn + 32, 0:n],
                 in0=s_ps[(b, tag)][:, first : first + n, :].rearrange("p t (j i) -> p j i t", j=4),
-                in1=tab[:, TAB_OFF[jn] : TAB_OFF[jn] + P * n].rearrange("p (j i t) -> p j i t", j=4, t=n),
+                in1=tab[jn][:].rearrange("p (j i) t -> p j i t", j=4),
                 op=ALU.mult,
             )
 
@@ -285,9 +284,10 @@ def tile_retentionhead_pa_t_kernel(tc, q, k, x, Wv, out):
                 load_x(g, False)
             transposes_x(b)
 
-        transposes_qk(0)
         tx_with_loads(0)
+        transposes_qk(0)
         scores(0, (3, 2, 1, 0))
+        copy0(0)
         transposes_qk(1)
 
         for i in range(0, B + 1):
@@ -298,8 +298,7 @@ def tile_retentionhead_pa_t_kernel(tc, q, k, x, Wv, out):
             if on(i):
                 if i == 0:
                     quant_wx(-2)
-                if i % 2 == 0:
-                    copy0(i)
+                    quant_wv()
                 weigh0(i)
                 if i == 0:
                     for jn in (3, 2, 1):
@@ -312,7 +311,7 @@ def tile_retentionhead_pa_t_kernel(tc, q, k, x, Wv, out):
                         weigh(i, jn)
                     if on(i + 1):
                         scores(i + 1, (1, 0) if jn == 1 else (jn,))
-                if on(i + 1) and i % 2 == 0:
+                if on(i + 1):
                     copy0(i + 1)
                 if i == 0:
                     tx_with_loads(2)

from contextlib import ExitStack
import math

import concourse.mybir as mybir
from concourse.masks import make_identity

F32 = mybir.dt.float32
BF16 = mybir.dt.bfloat16
U8 = mybir.dt.uint8
U32 = mybir.dt.uint32
I32 = mybir.dt.int32
FP8X4 = mybir.dt.float8_e4m3fn_x4
ALU = mybir.AluOpType
ACT = mybir.ActivationFunctionType

B, T, C, H = 32, 512, 512, 128
P = 128
GAMMA = 0.96875
FLOPS = 3 * 2 * B * T * T * H
PIN = True
BUFS = 2
AHEAD = 2


def tile_retentionhead_pa_t_kernel(tc, q, k, x, Wv, out):
    nc = tc.nc
    with ExitStack() as ctx:
        const = ctx.enter_context(tc.tile_pool(name="const", bufs=1))
        loads = ctx.enter_context(tc.tile_pool(name="loads", bufs=AHEAD + 2))
        work = ctx.enter_context(tc.tile_pool(name="work", bufs=3))
        outs = ctx.enter_context(tc.tile_pool(name="outs", bufs=3))
        psum = ctx.enter_context(tc.psum_pool(name="psum", bufs=1))
        if PIN:
            ctx.enter_context(tc.manual_schedule())

        x_in, q_in, k_in = {}, {}, {}

        def load_qk(g):
            kt = loads.tile([P, 2 * 512], BF16, name="kt", tag="kt")
            qt = loads.tile([P, 2 * 512], BF16, name="qt", tag="qt")
            bs = slice(2 * g, 2 * g + 2)
            k_in[g], q_in[g] = kt, qt
            if g == 0:
                return
            nc.sync.dma_start(
                out=kt[:].rearrange("p (b t h) -> p b t h", b=2, t=4),
                in_=k[bs].rearrange("b (t p) h -> p b t h", p=P),
            )
            nc.sync.dma_start(
                out=qt[:].rearrange("p (b w) -> p b w", b=2),
                in_=q[bs].rearrange("b (p j) h -> p b (j h)", j=4),
            )

        def load_qk_one(r):
            cols = slice(r * 512, (r + 1) * 512)
            nc.sync.dma_start(
                out=k_in[0][:, cols].rearrange("p (t h) -> p t h", t=4), in_=k[r].rearrange("(t p) h -> p t h", p=P)
            )
            nc.sync.dma_start(out=q_in[0][:, cols], in_=q[r].rearrange("(p j) h -> p (j h)", j=4))

        def load_x(g, split):
            xt = loads.tile([P, 2 * 2048], BF16, name="xt", tag="xt")
            x_in[g] = xt
            if split:
                for r in range(2):
                    nc.sync.dma_start(
                        out=xt[:, r * 2048 : (r + 1) * 2048],
                        in_=x[2 * g + r].rearrange("(p j) c -> p (j c)", j=4),
                    )
                    if g == 0:
                        load_qk_one(r)
                    if g == 0 and r == 0:
                        nc.sync.dma_start(
                            out=wv_sb[:].rearrange("q (u e) h -> q u e h", u=2),
                            in_=Wv.rearrange("(u q e) h -> q u e h", u=2, e=2),
                        )
            else:
                nc.sync.dma_start(
                    out=xt[:].rearrange("p (b w) -> p b w", b=2),
                    in_=x[2 * g : 2 * g + 2].rearrange("b (p j) c -> p b (j c)", j=4),
                )

        wv_sb = const.tile([P, 4, H], BF16, name="wv_sb")
        for g in range(AHEAD + 1):
            load_qk(g)
            load_x(g, g < 2)

        zeros = const.tile([P, P], BF16, name="zeros")
        nc.vector.memset(zeros[:].bitcast(I32), 0)
        idle = psum.tile([P, 4, P], F32, name="idle", tag="sa")
        for n in range(16):
            nc.tensor.matmul(out=idle[:, n % 4, :], lhsT=zeros[:], rhs=zeros[:], start=True, stop=True)
        warm_in = const.tile([P, 1], F32, name="warm_in")
        warm_out = const.tile([P, 1], F32, name="warm_out")
        nc.vector.memset(warm_in[:], 0.0)
        nc.scalar.activation(out=warm_out[:], in_=warm_in[:], func=ACT.Exp)
        d_f = const.tile([P, P], F32, name="d_f")
        nc.gpsimd.iota(
            out=d_f[:], pattern=[[1, 4], [4, 32]], base=0, channel_multiplier=-1, allow_small_or_imprecise_dtypes=True
        )
        off4 = const.tile([P, 4], F32, name="off4")
        nc.gpsimd.iota(
            out=off4[:], pattern=[[-P, 4]], base=3 * P, channel_multiplier=0, allow_small_or_imprecise_dtypes=True
        )
        ident_b = const.tile([P, P], BF16, name="ident_b")
        make_identity(nc, ident_b[:])
        ident_f = const.tile([P, P], F32, name="ident_f")
        make_identity(nc, ident_f[:])
        gwx = [const.tile([P, 4096], BF16, name="gwx%d" % n, align_bytes=64) for n in range(BUFS)]
        for n in range(BUFS):
            nc.gpsimd.memset(gwx[n][:, 0:2048].bitcast(I32), 0)

        dist = const.tile([P, P, 4], F32, name="dist")
        powers = const.tile([P, P, 4], F32, name="powers")
        tab = [const.tile([P, P, jn + 1], F32, name="tab%d" % jn) for jn in range(4)]
        nc.vector.tensor_tensor(
            out=dist[:],
            in0=d_f[:].unsqueeze(2).to_broadcast([P, P, 4]),
            in1=off4[:].unsqueeze(1).to_broadcast([P, P, 4]),
            op=ALU.add,
        )
        nc.scalar.activation(out=powers[:], in_=dist[:], func=ACT.Exp, scale=math.log(GAMMA), bias=-0.5 * math.log(C))
        nc.vector.scalar_tensor_tensor(
            out=tab[3][:], in0=dist[:], scalar=0.0, in1=powers[:], op0=ALU.is_ge, op1=ALU.mult
        )
        nc.scalar.copy(out=tab[0][:], in_=tab[3][:, :, 3:4])
        nc.vector.tensor_copy(out=tab[2][:], in_=tab[3][:, :, 1:4])
        nc.scalar.copy(out=tab[1][:], in_=tab[3][:, :, 2:4])

        g_wv = const.tile([P, H, 4], BF16, name="g_wv", align_bytes=64)
        wv_q = const.tile([P, H], U32, name="wv_q", align_bytes=64)
        wv_s = const.tile([P, H], U8, name="wv_s", align_bytes=64)

        def quant_wv():
            nc.vector.tensor_copy(out=g_wv[:], in_=wv_sb[:].rearrange("q t h -> q h t"))
            nc.vector.quantize_mx(
                out=wv_q[:].bitcast(FP8X4), scales=wv_s[:], in_=g_wv[:].rearrange("q h t -> q (h t)")
            )

        def on(b):
            return 0 <= b < B

        qkT, xq, xs, gv, vq, vs, wq, ws, s_ps = {}, {}, {}, {}, {}, {}, {}, {}, {}

        def transposes_qk(b):
            g, r = divmod(b, 2)
            qk_ps = psum.tile([P, 8, P], BF16, name="qk_ps", tag="qk")
            for t in range(4):
                nc.tensor.transpose(
                    out=qk_ps[:, t, :], in_=k_in[g][:, r * 512 + t * P : r * 512 + (t + 1) * P], identity=ident_b[:]
                )
            for j in range(4):
                nc.tensor.transpose(
                    out=qk_ps[:, 4 + j, :], in_=q_in[g][:, r * 512 + j * P : r * 512 + (j + 1) * P], identity=ident_b[:]
                )
            qkT[b] = work.tile([P, 8, P], BF16, name="qkT", tag="qkT")
            nc.scalar.copy(out=qkT[b][:], in_=qk_ps[:])

        def transposes_x(b):
            g, r = divmod(b, 2)
            xw = x_in[g][:].bitcast(F32)
            gx = gwx[(b - 2) % BUFS][:, 2048:4096]
            gxw = gx.bitcast(F32).rearrange("c (p hf s) -> c hf p s", hf=2, s=4)
            for hf in range(2):
                x_ps = psum.tile([P, 4, P], F32, name="x_ps%d" % hf, tag="x%d" % hf)
                for s in range(4):
                    j, u = 2 * hf + s // 2, s % 2
                    o = r * 1024 + j * 256 + u * P
                    nc.tensor.transpose(out=x_ps[:, s, :], in_=xw[:, o : o + P], identity=ident_f[:])
                copy = nc.vector.tensor_copy if hf == 1 and b < 3 else nc.scalar.copy
                copy(out=gxw[:, hf], in_=x_ps[:].rearrange("c s p -> c p s"))

        def quant_wx(i):
            lo, hi = (0 if on(i) else 512), (1024 if on(i + 2) else 512)
            codes = work.tile([P, 1024], U32, name="codes", tag="codes", align_bytes=64)
            scales = work.tile([P, 1024], U8, name="scales", tag="scales", align_bytes=64)
            step = 256 if i == B - 1 else hi - lo
            for c in range(lo, hi, step):
                cols = slice(c, c + step)
                nc.vector.quantize_mx(
                    out=codes[:, cols].bitcast(FP8X4),
                    scales=scales[:, cols],
                    in_=gwx[i % BUFS][:, 4 * c : 4 * (c + step)],
                )
            wq[i], ws[i] = codes[:, 0:512], scales[:, 0:512]
            xq[i + 2], xs[i + 2] = codes[:, 512:1024], scales[:, 512:1024]

        S_SLOT = {3: ("sa", 0), 2: ("sb", 0), 1: ("sc", 0), 0: ("sc", 2)}
        s0_sb = {}

        def scores(b, jns):
            for jn in jns:
                tag, first = S_SLOT[jn]
                if (b, tag) not in s_ps:
                    s_ps[(b, tag)] = psum.tile([P, 4, P], F32, name="s_" + tag, tag=tag)
                bank = s_ps[(b, tag)]
                for t in range(jn + 1):
                    nc.tensor.matmul(
                        out=bank[:, first + t, :].rearrange("p (j i) -> p j i", j=4),
                        lhsT=qkT[b][:, t, :],
                        rhs=qkT[b][:, 4:8, 32 * jn : 32 * jn + 32],
                        start=True,
                        stop=True,
                    )

        def copy0(b):
            s0_sb[b] = work.tile([P, P], F32, name="s0_sb", tag="s0_sb")
            nc.scalar.copy(out=s0_sb[b][:], in_=s_ps[(b, "sc")][:, 2, :])

        def weigh0(b):
            if on(b - 1):
                code = work.tile([P, 1], U32, name="code", tag="code")
                nc.gpsimd.tensor_copy(out=code[:], in_=wq[b - 1][:, 0:1])
            nc.gpsimd.tensor_tensor(
                out=gwx[b % BUFS][:, 0:2048].rearrange("p (j i t) -> p j i t", j=4, t=4)[:, :, 0:32, 0:1],
                in0=s0_sb[b][:].rearrange("p (j i t) -> p j i t", j=4, t=1),
                in1=tab[0][:].rearrange("p (j i) t -> p j i t", j=4),
                op=ALU.mult,
            )

        def weigh(b, jn):
            tag, first = S_SLOT[jn]
            n = jn + 1
            nc.vector.tensor_tensor(
                out=gwx[b % BUFS][:, 0:2048].rearrange("p (j i t) -> p j i t", j=4, t=4)[:, :, 32 * jn : 32 * jn + 32, 0:n],
                in0=s_ps[(b, tag)][:, first : first + n, :].rearrange("p t (j i) -> p j i t", j=4),
                in1=tab[jn][:].rearrange("p (j i) t -> p j i t", j=4),
                op=ALU.mult,
            )

        def values(b):
            v_ps = psum.tile([P, 4, H], F32, name="v_ps", tag="v")
            for t in range(4):
                cols = slice(t * P, (t + 1) * P)
                nc.tensor.matmul_mx(
                    out=v_ps[:, t, :],
                    lhsT=xq[b][:, cols].bitcast(FP8X4),
                    lhsT_scale=xs[b][:, cols],
                    rhs=wv_q[:].bitcast(FP8X4),
                    rhs_scale=wv_s[:],
                    start=True,
                    stop=True,
                )
            gv[b] = work.tile([P, H, 4], BF16, name="gv", tag="gv", align_bytes=64)
            nc.scalar.copy(out=gv[b][:], in_=v_ps[:].rearrange("p t h -> p h t"))

        def quant_v(b):
            vq[b] = work.tile([P, H], U32, name="vq", tag="vq", align_bytes=64)
            vs[b] = work.tile([P, H], U8, name="vs", tag="vs", align_bytes=64)
            nc.vector.quantize_mx(
                out=vq[b][:].bitcast(FP8X4), scales=vs[b][:], in_=gv[b][:].rearrange("p h t -> p (h t)")
            )

        def outputs(b):
            halves = [psum.tile([P, 4, H], F32, name="o_ps", tag="o")]
            halves.append(psum.tile([P, 4, H], F32, name="v_ps", tag="v") if b == B - 1 else halves[0])
            for j in range(4):
                cols = slice(j * P, (j + 1) * P)
                nc.tensor.matmul_mx(
                    out=halves[j // 2][:, j, :],
                    lhsT=wq[b][:, cols].bitcast(FP8X4),
                    lhsT_scale=ws[b][:, cols],
                    rhs=vq[b][:].bitcast(FP8X4),
                    rhs_scale=vs[b][:],
                    start=True,
                    stop=True,
                )
            o_sb = outs.tile([P, 4, H], F32, name="o_sb", tag="o_sb")
            out_b = out[b].rearrange("(i j) h -> i j h", j=4)
            if b < B - 1:
                nc.scalar.copy(out=o_sb[:], in_=halves[0][:])
                nc.sync.dma_start(out=out_b, in_=o_sb[:])
            else:
                o_sb2 = outs.tile([P, 2, H], F32, name="o_sb2", tag="o_sb2")
                nc.scalar.copy(out=o_sb[:, 0:2, :], in_=halves[0][:, 0:2, :])
                nc.vector.tensor_copy(out=o_sb2[:], in_=halves[1][:, 2:4, :])
                nc.sync.dma_start(out=out_b[:, 0:2, :], in_=o_sb[:, 0:2, :])
                nc.sync.dma_start(out=out_b[:, 2:4, :], in_=o_sb2[:])

        def tx_with_loads(b):
            g = b // 2 + AHEAD
            if b % 2 == 0 and b > 0 and g < B // 2:
                load_qk(g)
                load_x(g, False)
            transposes_x(b)

        tx_with_loads(0)
        transposes_qk(0)
        scores(0, (3, 2, 1, 0))
        copy0(0)
        transposes_qk(1)

        for i in range(0, B + 1):
            if i > 0:
                if on(i + 1):
                    values(i + 1)
                outputs(i - 1)
            if on(i):
                if i == 0:
                    quant_wx(-2)
                    quant_wv()
                weigh0(i)
                if i == 0:
                    for jn in (3, 2, 1):
                        weigh(i, jn)
                    tx_with_loads(1)
                    values(0)
                    quant_wx(-1)
                for jn in (3, 2, 1):
                    if i > 0:
                        weigh(i, jn)
                    if on(i + 1):
                        scores(i + 1, (1, 0) if jn == 1 else (jn,))
                if on(i + 1):
                    copy0(i + 1)
                if i == 0:
                    tx_with_loads(2)
                    values(1)
                if on(i + 2):
                    transposes_qk(i + 2)
                if on(i + 3):
                    tx_with_loads(i + 3)
                quant_v(i)
                quant_wx(i)
